import numpy as np
import ml_dtypes


def mxq(x, axis, fmt="e4m3"):
    dtype, down = {"e4m3": (ml_dtypes.float8_e4m3fn, 7), "e5m2": (ml_dtypes.float8_e5m2, 14)}[fmt]
    v = np.moveaxis(np.asarray(x, np.float32).astype(ml_dtypes.bfloat16).astype(np.float64), axis, -1)
    blocks = v.reshape(v.shape[:-1] + (-1, 32))
    amax = np.abs(blocks).max(-1, keepdims=True)
    byte = np.maximum(np.where(amax > 0, np.frexp(amax)[1] - 1 + 127, 0) - down, 1)
    scale = np.exp2(byte - 127.0)
    codes = (blocks / scale).astype(np.float32).astype(dtype).astype(np.float64)
    return np.moveaxis((codes * scale).reshape(v.shape), -1, axis)


WIDE = False


def mx_kscale(k):
    if not WIDE:
        return np.ones(k)
    levels = np.array([10, -10, 5, -5, 0])
    if k % 512:
        return np.exp2(np.random.permutation(np.resize(levels, k // 32))).repeat(32)
    a = np.empty((k // 512, 16))
    for p in range(k // 512):
        a[p, :8] = np.random.permutation(np.resize(levels, 8))
        for g in range(8):
            far = levels[np.abs(levels - a[p, g]) >= 10]
            a[p, g + 8] = far[np.random.randint(len(far))]
    return np.exp2(a.ravel()).repeat(32)


BF16 = ml_dtypes.bfloat16


def bf(x):
    return np.asarray(x, np.float32).astype(BF16)


def f64(x):
    return np.asarray(x).astype(np.float64)


B, S, H, NH = 16, 256, 512, 16
LN_EPS = 1e-5


def silu(v):
    return v / (1.0 + np.exp(-v))


def draw0():
    s, t = mx_kscale(H), mx_kscale(H)
    w = 1.0 / np.sqrt(H)
    z = (np.random.standard_normal((B, S, H)) + 0.3 * np.random.standard_normal((B, S, 1))) * 2.0 / S
    return {"z": bf(z),
            "hidden_states": bf(np.random.standard_normal((B, S, H)) * s),
            "Wg": bf(np.random.standard_normal((H, H)) * w / s[:, None]),
            "Wo": bf(np.random.standard_normal((H, H)) * w / t[:, None]),
            "gamma": bf((1.0 + 0.1 * np.random.standard_normal(H)) * t),
            "beta": bf(0.1 * np.random.standard_normal(H) * t)}


def core(z, hidden_states, Wg, Wo, gamma, beta):
    z = f64(z)
    g = mxq(f64(hidden_states), 2, "e4m3") @ mxq(f64(Wg), 0, "e4m3")
    mu = np.mean(z, axis=-1, keepdims=True)
    var = np.mean(np.square(z - mu), axis=-1, keepdims=True)
    zn = (z - mu) * (1.0 / np.sqrt(var + LN_EPS)) * f64(gamma) + f64(beta)
    h = zn * silu(g)
    return mxq(h, 2, "e4m3") @ mxq(f64(Wo), 0, "e4m3")


def e4m3fn_bytes(y):
    return np.clip(np.asarray(y, np.float64), -448.0, 448.0).astype(np.float32).astype(ml_dtypes.float8_e4m3fn).view(np.uint8)


def e4m3fn_values(b):
    return np.asarray(b, np.uint8).view(ml_dtypes.float8_e4m3fn).astype(np.float64)


def setup_inputs():
    d = draw0()
    x0 = np.asarray(d['hidden_states']).astype(np.float64)
    s = (np.max(np.abs(x0), axis=(0, 1), keepdims=True) / 448.0).astype(np.float32)
    out = {}
    for k, v in d.items():
        if k == 'hidden_states':
            out['hidden_states_bytes'] = e4m3fn_bytes(x0 / s.astype(np.float64))
            out['hidden_states_scale'] = s
        else:
            out[k] = v
    return out


def reference(z, hidden_states_bytes, hidden_states_scale, Wg, Wo, gamma, beta):
    return core(z, e4m3fn_values(hidden_states_bytes) * hidden_states_scale.astype(np.float64), Wg, Wo, gamma, beta)

@@ -1,0 +1,277 @@
+from contextlib import ExitStack
+
+import concourse.mybir as mybir
+from concourse.masks import make_identity
+
+TOKENS, H = 4096, 512
+FLOPS = 2 * 2 * TOKENS * H * H
+
+F32 = mybir.dt.float32
+BF16 = mybir.dt.bfloat16
+U32 = mybir.dt.uint32
+U8 = mybir.dt.uint8
+FP8 = mybir.dt.float8_e4m3fn
+FP8X4 = mybir.dt.float8_e4m3fn_x4
+ACT = mybir.ActivationFunctionType
+ALU = mybir.AluOpType
+
+P = 128
+PACK = 4
+SUB = 4
+GTOK = P * SUB
+GROUPS = TOKENS // GTOK
+EPS = 1e-5
+
+
+def tile_gatedlinearattention_pb_t_kernel(tc, z, hs_bytes, hs_scale, Wg, Wo, gamma, beta, out):
+    nc = tc.nc
+    z_v = z.flatten_outer_dims().rearrange("(g p i) d -> g p (i d)", p=P, i=SUB)
+    hs_v = hs_bytes.flatten_outer_dims().rearrange("(g p i) d -> g p (i d)", p=P, i=SUB)
+    out_v = out.flatten_outer_dims().rearrange("(g p i) d -> g p i d", p=P, i=SUB)
+
+    with ExitStack() as ctx:
+        keep = ctx.enter_context(tc.tile_pool(name="keep", bufs=1))
+        inp = ctx.enter_context(tc.tile_pool(name="inp", bufs=GROUPS))
+        work = ctx.enter_context(tc.tile_pool(name="work", bufs=2))
+        outp = ctx.enter_context(tc.tile_pool(name="outp", bufs=3))
+        ps_hs = ctx.enter_context(tc.psum_pool(name="ps_hs", bufs=2))
+        ps_g = ctx.enter_context(tc.psum_pool(name="ps_g", bufs=2))
+        ps_z = ctx.enter_context(tc.psum_pool(name="ps_z", bufs=2))
+        ps_o = ctx.enter_context(tc.psum_pool(name="ps_o", bufs=2))
+
+        hs_t = []
+        z_t = []
+        for g in range(GROUPS):
+            hb = inp.tile([P, SUB * H], U8, name="hb", align_bytes=64)
+            zb = inp.tile([P, SUB * H], BF16, name="zb", align_bytes=64)
+            hs_t.append(hb)
+            z_t.append(zb)
+        wg_raw = keep.tile([P, PACK, H], BF16, name="wg_raw", align_bytes=64)
+        wo_raw = keep.tile([P, PACK, H], BF16, name="wo_raw", align_bytes=64)
+        sc = keep.tile([P, PACK], F32, name="sc")
+        gam16 = keep.tile([P, PACK], BF16, name="gam16")
+        bet16 = keep.tile([P, PACK], BF16, name="bet16")
+        nc.sync.dma_start(out=hs_t[0][:], in_=hs_v[0])
+        nc.scalar.dma_start(out=sc[:], in_=hs_scale.rearrange("a b (p j) -> (a b p) j", j=PACK))
+        nc.scalar.dma_start(out=gam16[:], in_=gamma.rearrange("(p j) -> p j", j=PACK))
+        nc.scalar.dma_start(out=bet16[:], in_=beta.rearrange("(p j) -> p j", j=PACK))
+        nc.sync.dma_start(out=z_t[0][:], in_=z_v[0])
+        nc.sync.dma_start(out=wg_raw[:], in_=Wg.rearrange("(p j) c -> p j c", j=PACK))
+        nc.sync.dma_start(out=hs_t[1][:], in_=hs_v[1])
+        nc.sync.dma_start(out=z_t[1][:], in_=z_v[1])
+        nc.sync.dma_start(out=wo_raw[:], in_=Wo.rearrange("(p j) c -> p j c", j=PACK))
+        for g in range(2, GROUPS):
+            nc.sync.dma_start(out=hs_t[g][:], in_=hs_v[g])
+            nc.sync.dma_start(out=z_t[g][:], in_=z_v[g])
+
+        ident = keep.tile([P, P], F32, name="ident")
+        make_identity(nc, ident[:])
+        mhalf = keep.tile([P, SUB], F32, name="mhalf")
+        nc.gpsimd.memset(mhalf[:], -0.5)
+        dummy = keep.tile([P, 1], F32, name="dummy")
+        nc.gpsimd.memset(dummy[:], 0.0)
+        dummy2 = keep.tile([P, 1], F32, name="dummy2")
+        nc.scalar.activation(out=dummy2[:], in_=dummy[:], func=ACT.Silu)
+        gam = keep.tile([P, PACK], F32, name="gam")
+        bet = keep.tile([P, PACK], F32, name="bet")
+        nc.scalar.copy(out=gam[:], in_=gam16[:])
+        nc.scalar.copy(out=bet[:], in_=bet16[:])
+
+        wg_grp = keep.tile([P, H * PACK], BF16, name="wg_grp", align_bytes=64)
+        wo_grp = keep.tile([P, H * PACK], BF16, name="wo_grp", align_bytes=64)
+        wg_codes = keep.tile([P, H], U32, name="wg_codes", align_bytes=64)
+        wg_scales = keep.tile([P, H], U8, name="wg_scales", align_bytes=64)
+        wo_codes = keep.tile([P, H], U32, name="wo_codes", align_bytes=64)
+        wo_scales = keep.tile([P, H], U8, name="wo_scales", align_bytes=64)
+
+        def prep_wg():
+            nc.vector.tensor_copy(
+                out=wg_grp[:].rearrange("p (t m j) -> p t m j", t=PACK, j=PACK),
+                in_=wg_raw[:].rearrange("p j (m t) -> p t m j", t=PACK),
+            )
+            nc.vector.quantize_mx(out=wg_codes[:].bitcast(FP8X4), scales=wg_scales[:], in_=wg_grp[:])
+
+        def prep_wo():
+            nc.gpsimd.tensor_scalar(
+                out=wo_grp[:].rearrange("p (n j) -> p n j", j=PACK),
+                in0=wo_raw[:].rearrange("p j n -> p n j"),
+                scalar1=1.0, scalar2=0.0, op0=ALU.mult, op1=ALU.add,
+            )
+
+        def quant_wo():
+            nc.vector.quantize_mx(out=wo_codes[:].bitcast(FP8X4), scales=wo_scales[:], in_=wo_grp[:])
+
+        sc_b = sc[:].rearrange("p (u e) -> p u e", u=2).unsqueeze(1).to_broadcast([P, 256, 2, 2])
+
+        S = [dict() for g in range(GROUPS)]
+
+        shapes = {
+            "wide": ([P, SUB * H], BF16), "hsb": ([P, GTOK * PACK], BF16), "hc": ([P, GTOK], U32), "hsc": ([P, GTOK], U8),
+            "st": ([P, SUB, 6], F32), "nm": ([P, SUB], F32), "rs": ([P, SUB], F32), "zh": ([P, SUB, PACK, P], F32),
+            "sg": ([P, PACK, GTOK], F32), "zn": ([P, PACK, GTOK], F32), "hb": ([P, GTOK * PACK], BF16),
+            "c2": ([P, GTOK], U32), "s2": ([P, GTOK], U8), "o": ([P, SUB, H], F32), "tm": ([P, 6, SUB], F32),
+        }
+
+        def buf(g, key):
+            if key not in S[g]:
+                shape, dt = shapes[key]
+                pool = outp if key == "o" else work
+                S[g][key] = pool.tile(shape, dt, name=key, align_bytes=64)
+            return S[g][key]
+
+        def widen(g, i):
+            c = slice(i * H, (i + 1) * H)
+            nc.scalar.copy(out=buf(g, "wide")[:, c], in_=hs_t[g][:, c].bitcast(FP8))
+
+        def hs_turn(g, h):
+            words = buf(g, "wide")[:].bitcast(F32)
+            bank = ps_hs.tile([P, 2, 256], F32, name="hs_bank")
+            for i in range(2):
+                for u in range(2):
+                    w0 = (2 * h + i) * 256
+                    nc.tensor.transpose(bank[:, u, i * P : (i + 1) * P], words[:, w0 + u : w0 + 256 : 2], ident[:])
+            S[g]["hbank", h] = bank
+
+        def hs_prod(g, h):
+            bank = S[g]["hbank", h]
+            nc.vector.tensor_tensor(
+                out=buf(g, "hsb")[:, h * 1024 : (h + 1) * 1024].rearrange("p (n u e) -> p n u e", u=2, e=2),
+                in0=bank[:].bitcast(BF16).rearrange("p u (n e) -> p n u e", e=2),
+                in1=sc_b,
+                op=ALU.mult,
+            )
+
+        def hs_quant(g):
+            nc.vector.quantize_mx(out=buf(g, "hc")[:].bitcast(FP8X4), scales=buf(g, "hsc")[:], in_=buf(g, "hsb")[:])
+
+        def stats(g, i):
+            nc.vector.bn_stats(out=buf(g, "st")[:, i, :], in_=z_t[g][:, i * H : (i + 1) * H])
+
+        def moments(g):
+            st = buf(g, "st")
+            me, ve, mo, vo = st[:, :, 1], st[:, :, 2], st[:, :, 4], st[:, :, 5]
+            tm = buf(g, "tm")
+            nm, rs = buf(g, "nm"), buf(g, "rs")
+            gp = nc.gpsimd
+            gp.tensor_tensor(out=tm[:, 0, :], in0=me, in1=mo, op=ALU.add)
+            gp.tensor_tensor(out=tm[:, 1, :], in0=me, in1=mo, op=ALU.subtract)
+            gp.tensor_tensor(out=tm[:, 2, :], in0=ve, in1=vo, op=ALU.add)
+            gp.tensor_scalar(out=nm[:], in0=tm[:, 0, :], scalar1=-0.5, scalar2=0.0, op0=ALU.mult, op1=ALU.add)
+            gp.tensor_scalar(out=tm[:, 3, :], in0=tm[:, 1, :], scalar1=0.5, scalar2=0.0, op0=ALU.mult, op1=ALU.add)
+            gp.tensor_tensor(out=tm[:, 4, :], in0=tm[:, 3, :], in1=tm[:, 3, :], op=ALU.mult)
+            gp.tensor_scalar(out=tm[:, 5, :], in0=tm[:, 2, :], scalar1=1.0 / H, scalar2=EPS, op0=ALU.mult, op1=ALU.add)
+            gp.tensor_tensor(out=tm[:, 0, :], in0=tm[:, 4, :], in1=tm[:, 5, :], op=ALU.add)
+            gp.tensor_tensor(out=rs[:], in0=tm[:, 0, :], in1=mhalf[:], op=ALU.pow)
+
+        def center(g, i):
+            nc.gpsimd.tensor_scalar(
+                out=buf(g, "zh")[:, i, :, :],
+                in0=z_t[g][:, i * H : (i + 1) * H].rearrange("p (m t) -> p t m", t=PACK),
+                scalar1=buf(g, "nm")[:, i : i + 1], scalar2=buf(g, "rs")[:, i : i + 1],
+                op0=ALU.add, op1=ALU.mult,
+            )
+
+        def z_turn(g, t):
+            bank = ps_z.tile([P, GTOK], F32, name="z_bank")
+            for i in range(SUB):
+                nc.tensor.transpose(bank[:, i * P : (i + 1) * P], buf(g, "zh")[:, i, t, :], ident[:])
+            S[g]["zbank", t] = bank
+
+        def z_affine(g, t):
+            nc.scalar.activation(out=buf(g, "zn")[:, t, :], in_=S[g]["zbank", t][:], func=ACT.Identity,
+                                 scale=gam[:, t : t + 1], bias=bet[:, t : t + 1])
+
+        def gate_mm(g, t):
+            bank = ps_g.tile([P, GTOK], F32, name="g_bank")
+            nc.tensor.matmul_mx(
+                out=bank[:],
+                lhsT=wg_codes[:, t * P : (t + 1) * P].bitcast(FP8X4), lhsT_scale=wg_scales[:, t * P : (t + 1) * P],
+                rhs=buf(g, "hc")[:].bitcast(FP8X4), rhs_scale=buf(g, "hsc")[:],
+                start=True, stop=True,
+            )
+            S[g]["gbank", t] = bank
+
+        def gate_silu(g, t):
+            nc.scalar.activation(out=buf(g, "sg")[:, t, :], in_=S[g]["gbank", t][:], func=ACT.Silu)
+
+        def product(g, i):
+            n = slice(i * 2 * P, (i + 1) * 2 * P)
+            nc.vector.tensor_tensor(
+                out=buf(g, "hb")[:, i * 2 * P * PACK : (i + 1) * 2 * P * PACK].rearrange("p (c i t) -> p c t i", t=PACK, i=4),
+                in0=buf(g, "zn")[:, :, n].rearrange("p t (c i) -> p c t i", i=4),
+                in1=buf(g, "sg")[:, :, n].rearrange("p t (c i) -> p c t i", i=4),
+                op=ALU.mult,
+            )
+
+        def h_quant(g, j):
+            w = slice(j * 256, (j + 1) * 256)
+            nc.vector.quantize_mx(out=buf(g, "c2")[:, w].bitcast(FP8X4), scales=buf(g, "s2")[:, w],
+                                  in_=buf(g, "hb")[:, j * 1024 : (j + 1) * 1024])
+
+        def out_mm(g, i):
+            n = slice(i * P, (i + 1) * P)
+            bank = ps_o.tile([P, H], F32, name="o_bank")
+            nc.tensor.matmul_mx(
+                out=bank[:],
+                lhsT=buf(g, "c2")[:, n].bitcast(FP8X4), lhsT_scale=buf(g, "s2")[:, n],
+                rhs=wo_codes[:].bitcast(FP8X4), rhs_scale=wo_scales[:],
+                start=True, stop=True,
+            )
+            S[g]["obank", i] = bank
+
+        def out_copy(g, i, on_vector):
+            if on_vector:
+                nc.vector.tensor_copy(out=buf(g, "o")[:, i, :], in_=S[g]["obank", i][:])
+            else:
+                nc.scalar.copy(out=buf(g, "o")[:, i, :], in_=S[g]["obank", i][:])
+            if i % 2 == 1:
+                nc.sync.dma_start(out=out_v[g, :, i - 1 : i + 1, :], in_=buf(g, "o")[:, i - 1 : i + 1, :])
+
+        def ok(g):
+            return 0 <= g < GROUPS
+
+        VEC = {(7, 1), (7, 3), (6, 1), (6, 3), (5, 3), (5, 1), (4, 3), (3, 3)}
+        with tc.manual_schedule():
+            for s in range(-3, GROUPS + 1):
+                for k in range(4):
+                    a = s + 2
+                    if ok(a) and k < 2:
+                        hs_turn(a, k)
+                    if ok(s + 1):
+                        z_turn(s + 1, k)
+                        gate_mm(s + 1, k)
+                    if ok(s) and k >= 2:
+                        out_mm(s, k - 2)
+                    if ok(s - 1) and k < 2:
+                        out_mm(s - 1, k + 2)
+                    if ok(s + 3):
+                        stats(s + 3, k)
+                    if s == -2 and k == 1:
+                        prep_wg()
+                    if ok(a) and k < 2:
+                        hs_prod(a, k)
+                    if ok(s) and k % 2 == 0:
+                        product(s, k // 2)
+                    if ok(a) and k == 2:
+                        hs_quant(a)
+                    if ok(s) and k == 1:
+                        h_quant(s, 0)
+                    if s == 0 and k == 1:
+                        quant_wo()
+                    if ok(s) and k == 3:
+                        h_quant(s, 1)
+                    if ok(s + 3):
+                        widen(s + 3, k)
+                    if ok(s + 1):
+                        z_affine(s + 1, k)
+                        gate_silu(s + 1, k)
+                    if ok(s) and k >= 2:
+                        out_copy(s, k - 2, (s, k - 2) in VEC)
+                    if ok(s - 1) and k < 2:
+                        out_copy(s - 1, k + 2, (s - 1, k + 2) in VEC)
+                    if ok(a):
+                        if k == 0:
+                            moments(a)
+                        center(a, k)
+                    if s == -2 and k == 3:
+                        prep_wo()

@@ -164,7 +164,7 @@ def tile_gatedlinearattention_pb_t_kernel(tc, z, hs_bytes, hs_scale, Wg, Wo, gam
             gp.tensor_tensor(out=rs[:], in0=tm[:, 0, :], in1=mhalf[:], op=ALU.pow)
 
         def center(g, i):
-            nc.gpsimd.tensor_scalar(
+            nc.vector.tensor_scalar(
                 out=buf(g, "zh")[:, i, :, :],
                 in0=z_t[g][:, i * H : (i + 1) * H].rearrange("p (m t) -> p t m", t=PACK),
                 scalar1=buf(g, "nm")[:, i : i + 1], scalar2=buf(g, "rs")[:, i : i + 1],
@@ -183,7 +183,8 @@ def tile_gatedlinearattention_pb_t_kernel(tc, z, hs_bytes, hs_scale, Wg, Wo, gam
 
         def gate_mm(g, t):
             bank = ps_g.tile([P, GTOK], F32, name="g_bank")
-            nc.tensor.matmul_mx(
+            for r in range(2):
+              nc.tensor.matmul_mx(
                 out=bank[:],
                 lhsT=wg_codes[:, t * P : (t + 1) * P].bitcast(FP8X4), lhsT_scale=wg_scales[:, t * P : (t + 1) * P],
                 rhs=buf(g, "hc")[:].bitcast(FP8X4), rhs_scale=buf(g, "hsc")[:],
@@ -197,9 +198,9 @@ def tile_gatedlinearattention_pb_t_kernel(tc, z, hs_bytes, hs_scale, Wg, Wo, gam
         def product(g, i):
             n = slice(i * 2 * P, (i + 1) * 2 * P)
             nc.vector.tensor_tensor(
-                out=buf(g, "hb")[:, i * 2 * P * PACK : (i + 1) * 2 * P * PACK].rearrange("p (c i t) -> p c t i", t=PACK, i=4),
-                in0=buf(g, "zn")[:, :, n].rearrange("p t (c i) -> p c t i", i=4),
-                in1=buf(g, "sg")[:, :, n].rearrange("p t (c i) -> p c t i", i=4),
+                out=buf(g, "hb")[:, i * 2 * P * PACK : (i + 1) * 2 * P * PACK].rearrange("p (n t) -> p n t", t=PACK),
+                in0=buf(g, "zn")[:, :, n].rearrange("p t n -> p n t"),
+                in1=buf(g, "sg")[:, :, n].rearrange("p t n -> p n t"),
                 op=ALU.mult,
             )
 
@@ -230,7 +231,7 @@ def tile_gatedlinearattention_pb_t_kernel(tc, z, hs_bytes, hs_scale, Wg, Wo, gam
         def ok(g):
             return 0 <= g < GROUPS
 
-        VEC = {(7, 1), (7, 3), (6, 1), (6, 3), (5, 3), (5, 1), (4, 3), (3, 3)}
+        VEC = {(7, 1), (7, 3)}
         with tc.manual_schedule():
             for s in range(-3, GROUPS + 1):
                 for k in range(4):
@@ -244,6 +245,8 @@ def tile_gatedlinearattention_pb_t_kernel(tc, z, hs_bytes, hs_scale, Wg, Wo, gam
                         out_mm(s, k - 2)
                     if ok(s - 1) and k < 2:
                         out_mm(s - 1, k + 2)
+                    if ok(a) and k == 0:
+                        moments(a)
                     if ok(s + 3):
                         stats(s + 3, k)
                     if s == -2 and k == 1:
@@ -252,6 +255,9 @@ def tile_gatedlinearattention_pb_t_kernel(tc, z, hs_bytes, hs_scale, Wg, Wo, gam
                         hs_prod(a, k)
                     if ok(s) and k % 2 == 0:
                         product(s, k // 2)
+                    if ok(a) and k >= 2:
+                        center(a, 2 * k - 4)
+                        center(a, 2 * k - 3)
                     if ok(a) and k == 2:
                         hs_quant(a)
                     if ok(s) and k == 1:
@@ -269,9 +275,5 @@ def tile_gatedlinearattention_pb_t_kernel(tc, z, hs_bytes, hs_scale, Wg, Wo, gam
                         out_copy(s, k - 2, (s, k - 2) in VEC)
                     if ok(s - 1) and k < 2:
                         out_copy(s - 1, k + 2, (s - 1, k + 2) in VEC)
-                    if ok(a):
-                        if k == 0:
-                            moments(a)
-                        center(a, k)
                     if s == -2 and k == 3:
                         prep_wo()

@@ -21,6 +21,7 @@ SUB = 4
 GTOK = P * SUB
 GROUPS = TOKENS // GTOK
 EPS = 1e-5
+S_CENTER = 3
 
 
 def tile_gatedlinearattention_pb_t_kernel(tc, z, hs_bytes, hs_scale, Wg, Wo, gamma, beta, out):
@@ -51,18 +52,22 @@ def tile_gatedlinearattention_pb_t_kernel(tc, z, hs_bytes, hs_scale, Wg, Wo, gam
         sc = keep.tile([P, PACK], F32, name="sc")
         gam16 = keep.tile([P, PACK], BF16, name="gam16")
         bet16 = keep.tile([P, PACK], BF16, name="bet16")
+        half = SUB * H // 2
+        nc.sync.dma_start(out=z_t[0][:, :half], in_=z_v[0, :, :half])
         nc.sync.dma_start(out=hs_t[0][:], in_=hs_v[0])
         nc.scalar.dma_start(out=sc[:], in_=hs_scale.rearrange("a b (p j) -> (a b p) j", j=PACK))
         nc.scalar.dma_start(out=gam16[:], in_=gamma.rearrange("(p j) -> p j", j=PACK))
         nc.scalar.dma_start(out=bet16[:], in_=beta.rearrange("(p j) -> p j", j=PACK))
-        nc.sync.dma_start(out=z_t[0][:], in_=z_v[0])
+        nc.sync.dma_start(out=z_t[0][:, half:], in_=z_v[0, :, half:])
         nc.sync.dma_start(out=wg_raw[:], in_=Wg.rearrange("(p j) c -> p j c", j=PACK))
-        nc.sync.dma_start(out=hs_t[1][:], in_=hs_v[1])
         nc.sync.dma_start(out=z_t[1][:], in_=z_v[1])
+        nc.sync.dma_start(out=hs_t[1][:], in_=hs_v[1])
+        nc.sync.dma_start(out=z_t[2][:], in_=z_v[2])
+        nc.sync.dma_start(out=hs_t[2][:], in_=hs_v[2])
         nc.sync.dma_start(out=wo_raw[:], in_=Wo.rearrange("(p j) c -> p j c", j=PACK))
-        for g in range(2, GROUPS):
-            nc.sync.dma_start(out=hs_t[g][:], in_=hs_v[g])
+        for g in range(3, GROUPS):
             nc.sync.dma_start(out=z_t[g][:], in_=z_v[g])
+            nc.sync.dma_start(out=hs_t[g][:], in_=hs_v[g])
 
         ident = keep.tile([P, P], F32, name="ident")
         make_identity(nc, ident[:])
@@ -85,10 +90,12 @@ def tile_gatedlinearattention_pb_t_kernel(tc, z, hs_bytes, hs_scale, Wg, Wo, gam
         wo_scales = keep.tile([P, H], U8, name="wo_scales", align_bytes=64)
 
         def prep_wg():
-            nc.vector.tensor_copy(
+            nc.scalar.copy(
                 out=wg_grp[:].rearrange("p (t m j) -> p t m j", t=PACK, j=PACK),
                 in_=wg_raw[:].rearrange("p j (m t) -> p t m j", t=PACK),
             )
+
+        def quant_wg():
             nc.vector.quantize_mx(out=wg_codes[:].bitcast(FP8X4), scales=wg_scales[:], in_=wg_grp[:])
 
         def prep_wo():
@@ -107,7 +114,7 @@ def tile_gatedlinearattention_pb_t_kernel(tc, z, hs_bytes, hs_scale, Wg, Wo, gam
 
         shapes = {
             "wide": ([P, SUB * H], BF16), "hsb": ([P, GTOK * PACK], BF16), "hc": ([P, GTOK], U32), "hsc": ([P, GTOK], U8),
-            "st": ([P, SUB, 6], F32), "nm": ([P, SUB], F32), "rs": ([P, SUB], F32), "zh": ([P, SUB, PACK, P], F32),
+            "st": ([P, SUB, 6], F32), "nm": ([P, SUB], F32), "rs": ([P, SUB], F32), "nr": ([P, SUB], F32), "zh": ([P, SUB, PACK, P], F32),
             "sg": ([P, PACK, GTOK], F32), "zn": ([P, PACK, GTOK], F32), "hb": ([P, GTOK * PACK], BF16),
             "c2": ([P, GTOK], U32), "s2": ([P, GTOK], U8), "o": ([P, SUB, H], F32), "tm": ([P, 6, SUB], F32),
         }
@@ -162,8 +169,17 @@ def tile_gatedlinearattention_pb_t_kernel(tc, z, hs_bytes, hs_scale, Wg, Wo, gam
             gp.tensor_scalar(out=tm[:, 5, :], in0=tm[:, 2, :], scalar1=1.0 / H, scalar2=EPS, op0=ALU.mult, op1=ALU.add)
             gp.tensor_tensor(out=tm[:, 0, :], in0=tm[:, 4, :], in1=tm[:, 5, :], op=ALU.add)
             gp.tensor_tensor(out=rs[:], in0=tm[:, 0, :], in1=mhalf[:], op=ALU.pow)
+            if g < S_CENTER:
+                gp.tensor_tensor(out=buf(g, "nr")[:], in0=nm[:], in1=rs[:], op=ALU.mult)
 
         def center(g, i):
+            if g < S_CENTER:
+                nc.scalar.activation(
+                    out=buf(g, "zh")[:, i, :, :],
+                    in_=z_t[g][:, i * H : (i + 1) * H].rearrange("p (m t) -> p t m", t=PACK),
+                    func=ACT.Identity, scale=buf(g, "rs")[:, i : i + 1], bias=buf(g, "nr")[:, i : i + 1],
+                )
+                return
             nc.vector.tensor_scalar(
                 out=buf(g, "zh")[:, i, :, :],
                 in0=z_t[g][:, i * H : (i + 1) * H].rearrange("p (m t) -> p t m", t=PACK),
@@ -198,9 +214,9 @@ def tile_gatedlinearattention_pb_t_kernel(tc, z, hs_bytes, hs_scale, Wg, Wo, gam
         def product(g, i):
             n = slice(i * 2 * P, (i + 1) * 2 * P)
             nc.vector.tensor_tensor(
-                out=buf(g, "hb")[:, i * 2 * P * PACK : (i + 1) * 2 * P * PACK].rearrange("p (n t) -> p n t", t=PACK),
-                in0=buf(g, "zn")[:, :, n].rearrange("p t n -> p n t"),
-                in1=buf(g, "sg")[:, :, n].rearrange("p t n -> p n t"),
+                out=buf(g, "hb")[:, i * 2 * P * PACK : (i + 1) * 2 * P * PACK].rearrange("p (c i t) -> p c t i", i=2, t=PACK),
+                in0=buf(g, "zn")[:, :, n].rearrange("p t (c i) -> p c t i", i=2),
+                in1=buf(g, "sg")[:, :, n].rearrange("p t (c i) -> p c t i", i=2),
                 op=ALU.mult,
             )
 
@@ -247,11 +263,13 @@ def tile_gatedlinearattention_pb_t_kernel(tc, z, hs_bytes, hs_scale, Wg, Wo, gam
                         out_mm(s - 1, k + 2)
                     if ok(a) and k == 0:
                         moments(a)
+                    if ok(a) and k < 2 and s < 0:
+                        hs_prod(a, k)
                     if ok(s + 3):
                         stats(s + 3, k)
-                    if s == -2 and k == 1:
-                        prep_wg()
-                    if ok(a) and k < 2:
+                    if s == -2 and k == 3:
+                        quant_wg()
+                    if ok(a) and k < 2 and s >= 0:
                         hs_prod(a, k)
                     if ok(s) and k % 2 == 0:
                         product(s, k // 2)
@@ -268,6 +286,8 @@ def tile_gatedlinearattention_pb_t_kernel(tc, z, hs_bytes, hs_scale, Wg, Wo, gam
                         h_quant(s, 1)
                     if ok(s + 3):
                         widen(s + 3, k)
+                    if s == -3 and k == 3:
+                        prep_wg()
                     if ok(s + 1):
                         z_affine(s + 1, k)
                         gate_silu(s + 1, k)

@@ -17,70 +17,68 @@ ALU = mybir.AluOpType
 
 P = 128
 PACK = 4
-SUB = 4
-GTOK = P * SUB
-GROUPS = TOKENS // GTOK
 EPS = 1e-5
-S_CENTER = 3
+SIZES = [2, 4, 4, 4, 4, 4, 4, 4, 2]
+NG = len(SIZES)
+S_CENTER = 8
+GATE_REPEAT = 2
+V_COPY = {(8, 1)}
 
 
 def tile_gatedlinearattention_pb_t_kernel(tc, z, hs_bytes, hs_scale, Wg, Wo, gamma, beta, out):
     nc = tc.nc
-    z_v = z.flatten_outer_dims().rearrange("(g p i) d -> g p (i d)", p=P, i=SUB)
-    hs_v = hs_bytes.flatten_outer_dims().rearrange("(g p i) d -> g p (i d)", p=P, i=SUB)
-    out_v = out.flatten_outer_dims().rearrange("(g p i) d -> g p i d", p=P, i=SUB)
+    z2 = z.flatten_outer_dims()
+    hs2 = hs_bytes.flatten_outer_dims()
+    out2 = out.flatten_outer_dims()
+    starts = [sum(SIZES[:g]) * P for g in range(NG)]
+
+    def rows(x, g):
+        n = SIZES[g]
+        return x[starts[g] : starts[g] + n * P, :].rearrange("(p i) d -> p i d", i=n)
 
     with ExitStack() as ctx:
         keep = ctx.enter_context(tc.tile_pool(name="keep", bufs=1))
-        inp = ctx.enter_context(tc.tile_pool(name="inp", bufs=GROUPS))
-        work = ctx.enter_context(tc.tile_pool(name="work", bufs=2))
+        inp = ctx.enter_context(tc.tile_pool(name="inp", bufs=NG))
+        work = ctx.enter_context(tc.tile_pool(name="work", bufs=3))
         outp = ctx.enter_context(tc.tile_pool(name="outp", bufs=3))
         ps_hs = ctx.enter_context(tc.psum_pool(name="ps_hs", bufs=2))
         ps_g = ctx.enter_context(tc.psum_pool(name="ps_g", bufs=2))
         ps_z = ctx.enter_context(tc.psum_pool(name="ps_z", bufs=2))
         ps_o = ctx.enter_context(tc.psum_pool(name="ps_o", bufs=2))
 
-        hs_t = []
-        z_t = []
-        for g in range(GROUPS):
-            hb = inp.tile([P, SUB * H], U8, name="hb", align_bytes=64)
-            zb = inp.tile([P, SUB * H], BF16, name="zb", align_bytes=64)
-            hs_t.append(hb)
-            z_t.append(zb)
-        wg_raw = keep.tile([P, PACK, H], BF16, name="wg_raw", align_bytes=64)
-        wo_raw = keep.tile([P, PACK, H], BF16, name="wo_raw", align_bytes=64)
-        sc = keep.tile([P, PACK], F32, name="sc")
+        sc4 = keep.tile([P, PACK], F32, name="sc4")
         gam16 = keep.tile([P, PACK], BF16, name="gam16")
         bet16 = keep.tile([P, PACK], BF16, name="bet16")
-        half = SUB * H // 2
-        nc.sync.dma_start(out=z_t[0][:, :half], in_=z_v[0, :, :half])
-        nc.sync.dma_start(out=hs_t[0][:], in_=hs_v[0])
-        nc.scalar.dma_start(out=sc[:], in_=hs_scale.rearrange("a b (p j) -> (a b p) j", j=PACK))
-        nc.scalar.dma_start(out=gam16[:], in_=gamma.rearrange("(p j) -> p j", j=PACK))
-        nc.scalar.dma_start(out=bet16[:], in_=beta.rearrange("(p j) -> p j", j=PACK))
-        nc.sync.dma_start(out=z_t[0][:, half:], in_=z_v[0, :, half:])
-        nc.sync.dma_start(out=wg_raw[:], in_=Wg.rearrange("(p j) c -> p j c", j=PACK))
-        nc.sync.dma_start(out=z_t[1][:], in_=z_v[1])
-        nc.sync.dma_start(out=hs_t[1][:], in_=hs_v[1])
-        nc.sync.dma_start(out=z_t[2][:], in_=z_v[2])
-        nc.sync.dma_start(out=hs_t[2][:], in_=hs_v[2])
-        nc.sync.dma_start(out=wo_raw[:], in_=Wo.rearrange("(p j) c -> p j c", j=PACK))
-        for g in range(3, GROUPS):
-            nc.sync.dma_start(out=z_t[g][:], in_=z_v[g])
-            nc.sync.dma_start(out=hs_t[g][:], in_=hs_v[g])
+        wg_raw = keep.tile([P, PACK, H], BF16, name="wg_raw", align_bytes=64)
+        wo_raw = keep.tile([P, PACK, H], BF16, name="wo_raw", align_bytes=64)
+        hs_t, z_t = [], []
+        for g in range(NG):
+            hs_b = inp.tile([P, SIZES[g], H], U8, name="hs_b", align_bytes=64)
+            z_b = inp.tile([P, SIZES[g], H], BF16, name="z_b", align_bytes=64)
+            hs_t.append(hs_b)
+            z_t.append(z_b)
+        nc.scalar.dma_start(out=sc4[:], in_=hs_scale.rearrange("a b (p j) -> (a b p) j", j=PACK))
+        for g in range(NG):
+            nc.sync.dma_start(out=z_t[g][:], in_=rows(z2, g))
+            nc.sync.dma_start(out=hs_t[g][:], in_=rows(hs2, g))
+            if g == 0:
+                nc.sync.dma_start(out=wg_raw[:], in_=Wg.rearrange("(p j) c -> p j c", j=PACK))
+                nc.scalar.dma_start(out=gam16[:], in_=gamma.rearrange("(p j) -> p j", j=PACK))
+                nc.scalar.dma_start(out=bet16[:], in_=beta.rearrange("(p j) -> p j", j=PACK))
+            if g == 1:
+                nc.sync.dma_start(out=wo_raw[:], in_=Wo.rearrange("(p j) c -> p j c", j=PACK))
 
         ident = keep.tile([P, P], F32, name="ident")
         make_identity(nc, ident[:])
-        mhalf = keep.tile([P, SUB], F32, name="mhalf")
+        mhalf = keep.tile([P, PACK], F32, name="mhalf")
         nc.gpsimd.memset(mhalf[:], -0.5)
         dummy = keep.tile([P, 1], F32, name="dummy")
-        nc.gpsimd.memset(dummy[:], 0.0)
+        nc.vector.memset(dummy[:], 0.0)
         dummy2 = keep.tile([P, 1], F32, name="dummy2")
         nc.scalar.activation(out=dummy2[:], in_=dummy[:], func=ACT.Silu)
         gam = keep.tile([P, PACK], F32, name="gam")
         bet = keep.tile([P, PACK], F32, name="bet")
-        nc.scalar.copy(out=gam[:], in_=gam16[:])
-        nc.scalar.copy(out=bet[:], in_=bet16[:])
+        sc_t = keep.tile([P, H], F32, name="sc_t", align_bytes=64)
 
         wg_grp = keep.tile([P, H * PACK], BF16, name="wg_grp", align_bytes=64)
         wo_grp = keep.tile([P, H * PACK], BF16, name="wo_grp", align_bytes=64)
@@ -89,10 +87,16 @@ def tile_gatedlinearattention_pb_t_kernel(tc, z, hs_bytes, hs_scale, Wg, Wo, gam
         wo_codes = keep.tile([P, H], U32, name="wo_codes", align_bytes=64)
         wo_scales = keep.tile([P, H], U8, name="wo_scales", align_bytes=64)
 
-        def prep_wg():
+        def spread_scale():
+            bank = ps_hs.tile([P, PACK, P], F32, name="hs_bank")
+            for j in range(PACK):
+                nc.tensor.transpose(bank[:, j, :], sc4[:, j : j + 1].to_broadcast([P, P]), ident[:])
+            nc.scalar.copy(out=sc_t[:].rearrange("p (n j) -> p n j", j=PACK), in_=bank[:].rearrange("p j n -> p n j"))
+
+        def prep_wg(h):
             nc.scalar.copy(
-                out=wg_grp[:].rearrange("p (t m j) -> p t m j", t=PACK, j=PACK),
-                in_=wg_raw[:].rearrange("p j (m t) -> p t m j", t=PACK),
+                out=wg_grp[:, h * 1024 : (h + 1) * 1024].rearrange("p (t m j) -> p t m j", t=2, j=PACK),
+                in_=wg_raw[:].rearrange("p j (m t) -> p t m j", t=PACK)[:, 2 * h : 2 * h + 2],
             )
 
         def quant_wg():
@@ -108,113 +112,104 @@ def tile_gatedlinearattention_pb_t_kernel(tc, z, hs_bytes, hs_scale, Wg, Wo, gam
         def quant_wo():
             nc.vector.quantize_mx(out=wo_codes[:].bitcast(FP8X4), scales=wo_scales[:], in_=wo_grp[:])
 
-        sc_b = sc[:].rearrange("p (u e) -> p u e", u=2).unsqueeze(1).to_broadcast([P, 256, 2, 2])
-
-        S = [dict() for g in range(GROUPS)]
-
+        G = [dict() for g in range(NG)]
         shapes = {
-            "wide": ([P, SUB * H], BF16), "hsb": ([P, GTOK * PACK], BF16), "hc": ([P, GTOK], U32), "hsc": ([P, GTOK], U8),
-            "st": ([P, SUB, 6], F32), "nm": ([P, SUB], F32), "rs": ([P, SUB], F32), "nr": ([P, SUB], F32), "zh": ([P, SUB, PACK, P], F32),
-            "sg": ([P, PACK, GTOK], F32), "zn": ([P, PACK, GTOK], F32), "hb": ([P, GTOK * PACK], BF16),
-            "c2": ([P, GTOK], U32), "s2": ([P, GTOK], U8), "o": ([P, SUB, H], F32), "tm": ([P, 6, SUB], F32),
+            "hsm": ([P, 4, H], BF16), "hsb": ([P, 4 * H], BF16), "hc": ([P, H], U32), "hsc": ([P, H], U8),
+            "st": ([P, 4, 6], F32), "nm": ([P, 4], F32), "rs": ([P, 4], F32), "nr": ([P, 4], F32), "mv": ([P, 4, 2], F32), "ve": ([P, 4], F32),
+            "zh": ([P, 4, PACK, P], F32), "sg": ([P, PACK, H], F32), "zn": ([P, PACK, H], F32),
+            "hb": ([P, 4 * H], BF16), "c2": ([P, H], U32), "s2": ([P, H], U8), "o": ([P, 4, H], F32),
         }
 
         def buf(g, key):
-            if key not in S[g]:
+            if key not in G[g]:
                 shape, dt = shapes[key]
                 pool = outp if key == "o" else work
-                S[g][key] = pool.tile(shape, dt, name=key, align_bytes=64)
-            return S[g][key]
+                G[g][key] = pool.tile(shape, dt, name=key, align_bytes=64)
+            return G[g][key]
 
-        def widen(g, i):
-            c = slice(i * H, (i + 1) * H)
-            nc.scalar.copy(out=buf(g, "wide")[:, c], in_=hs_t[g][:, c].bitcast(FP8))
+        def stats(g, i):
+            nc.vector.bn_stats(out=buf(g, "st")[:, i, :], in_=z_t[g][:, i, :])
+
+        def on_scalar(g, i):
+            return starts[g] // P + i < S_CENTER
+
+        def aggregate(g):
+            for i in range(SIZES[g]):
+                nc.vector.bn_aggr(out=buf(g, "mv")[:, i, :], in_=buf(g, "st")[:, i, :])
+
+        def moments(g):
+            n = SIZES[g]
+            mean, var = buf(g, "mv")[:, :n, 0], buf(g, "mv")[:, :n, 1]
+            ve, rs = buf(g, "ve")[:, :n], buf(g, "rs")[:, :n]
+            nc.gpsimd.tensor_scalar(out=ve, in0=var, scalar1=1.0, scalar2=EPS, op0=ALU.mult, op1=ALU.add)
+            nc.gpsimd.tensor_tensor(out=rs, in0=ve, in1=mhalf[:, :n], op=ALU.pow)
+            if on_scalar(g, 0):
+                nm, nr = buf(g, "nm")[:, :n], buf(g, "nr")[:, :n]
+                nc.gpsimd.tensor_scalar(out=nm, in0=mean, scalar1=-1.0, scalar2=0.0, op0=ALU.mult, op1=ALU.add)
+                nc.gpsimd.tensor_tensor(out=nr, in0=nm, in1=rs, op=ALU.mult)
+
+        def center(g, i):
+            src = z_t[g][:, i, :].rearrange("p (m t) -> p t m", t=PACK)
+            dst = buf(g, "zh")[:, i, :, :]
+            if on_scalar(g, i):
+                nc.scalar.activation(out=dst, in_=src, func=ACT.Identity,
+                                     scale=buf(g, "rs")[:, i : i + 1], bias=buf(g, "nr")[:, i : i + 1])
+            else:
+                nc.vector.tensor_scalar(out=dst, in0=src, scalar1=buf(g, "mv")[:, i, 0:1], scalar2=buf(g, "rs")[:, i : i + 1],
+                                        op0=ALU.subtract, op1=ALU.mult)
+
+        def hs_prod(g, i):
+            nc.vector.tensor_tensor(out=buf(g, "hsm")[:, i, :], in0=hs_t[g][:, i, :].bitcast(FP8), in1=sc_t[:], op=ALU.mult)
 
         def hs_turn(g, h):
-            words = buf(g, "wide")[:].bitcast(F32)
             bank = ps_hs.tile([P, 2, 256], F32, name="hs_bank")
             for i in range(2):
+                words = buf(g, "hsm")[:, 2 * h + i, :].bitcast(F32)
                 for u in range(2):
-                    w0 = (2 * h + i) * 256
-                    nc.tensor.transpose(bank[:, u, i * P : (i + 1) * P], words[:, w0 + u : w0 + 256 : 2], ident[:])
-            S[g]["hbank", h] = bank
+                    nc.tensor.transpose(bank[:, u, i * P : (i + 1) * P], words[:, u:256:2], ident[:])
+            G[g]["hbank", h] = bank
 
-        def hs_prod(g, h):
-            bank = S[g]["hbank", h]
-            nc.vector.tensor_tensor(
-                out=buf(g, "hsb")[:, h * 1024 : (h + 1) * 1024].rearrange("p (n u e) -> p n u e", u=2, e=2),
-                in0=bank[:].bitcast(BF16).rearrange("p u (n e) -> p n u e", e=2),
-                in1=sc_b,
-                op=ALU.mult,
+        def hs_copy(g, h):
+            nc.scalar.copy(
+                out=buf(g, "hsb")[:, h * 1024 : (h + 1) * 1024].bitcast(F32).rearrange("p (n u) -> p n u", u=2),
+                in_=G[g]["hbank", h][:].rearrange("p u n -> p n u"),
             )
 
         def hs_quant(g):
-            nc.vector.quantize_mx(out=buf(g, "hc")[:].bitcast(FP8X4), scales=buf(g, "hsc")[:], in_=buf(g, "hsb")[:])
-
-        def stats(g, i):
-            nc.vector.bn_stats(out=buf(g, "st")[:, i, :], in_=z_t[g][:, i * H : (i + 1) * H])
-
-        def moments(g):
-            st = buf(g, "st")
-            me, ve, mo, vo = st[:, :, 1], st[:, :, 2], st[:, :, 4], st[:, :, 5]
-            tm = buf(g, "tm")
-            nm, rs = buf(g, "nm"), buf(g, "rs")
-            gp = nc.gpsimd
-            gp.tensor_tensor(out=tm[:, 0, :], in0=me, in1=mo, op=ALU.add)
-            gp.tensor_tensor(out=tm[:, 1, :], in0=me, in1=mo, op=ALU.subtract)
-            gp.tensor_tensor(out=tm[:, 2, :], in0=ve, in1=vo, op=ALU.add)
-            gp.tensor_scalar(out=nm[:], in0=tm[:, 0, :], scalar1=-0.5, scalar2=0.0, op0=ALU.mult, op1=ALU.add)
-            gp.tensor_scalar(out=tm[:, 3, :], in0=tm[:, 1, :], scalar1=0.5, scalar2=0.0, op0=ALU.mult, op1=ALU.add)
-            gp.tensor_tensor(out=tm[:, 4, :], in0=tm[:, 3, :], in1=tm[:, 3, :], op=ALU.mult)
-            gp.tensor_scalar(out=tm[:, 5, :], in0=tm[:, 2, :], scalar1=1.0 / H, scalar2=EPS, op0=ALU.mult, op1=ALU.add)
-            gp.tensor_tensor(out=tm[:, 0, :], in0=tm[:, 4, :], in1=tm[:, 5, :], op=ALU.add)
-            gp.tensor_tensor(out=rs[:], in0=tm[:, 0, :], in1=mhalf[:], op=ALU.pow)
-            if g < S_CENTER:
-                gp.tensor_tensor(out=buf(g, "nr")[:], in0=nm[:], in1=rs[:], op=ALU.mult)
-
-        def center(g, i):
-            if g < S_CENTER:
-                nc.scalar.activation(
-                    out=buf(g, "zh")[:, i, :, :],
-                    in_=z_t[g][:, i * H : (i + 1) * H].rearrange("p (m t) -> p t m", t=PACK),
-                    func=ACT.Identity, scale=buf(g, "rs")[:, i : i + 1], bias=buf(g, "nr")[:, i : i + 1],
-                )
-                return
-            nc.vector.tensor_scalar(
-                out=buf(g, "zh")[:, i, :, :],
-                in0=z_t[g][:, i * H : (i + 1) * H].rearrange("p (m t) -> p t m", t=PACK),
-                scalar1=buf(g, "nm")[:, i : i + 1], scalar2=buf(g, "rs")[:, i : i + 1],
-                op0=ALU.add, op1=ALU.mult,
-            )
+            n = SIZES[g] * P
+            nc.vector.quantize_mx(out=buf(g, "hc")[:, :n].bitcast(FP8X4), scales=buf(g, "hsc")[:, :n], in_=buf(g, "hsb")[:, : 4 * n])
 
         def z_turn(g, t):
-            bank = ps_z.tile([P, GTOK], F32, name="z_bank")
-            for i in range(SUB):
+            bank = ps_z.tile([P, H], F32, name="z_bank")
+            for i in range(SIZES[g]):
                 nc.tensor.transpose(bank[:, i * P : (i + 1) * P], buf(g, "zh")[:, i, t, :], ident[:])
-            S[g]["zbank", t] = bank
+            G[g]["zbank", t] = bank
 
         def z_affine(g, t):
-            nc.scalar.activation(out=buf(g, "zn")[:, t, :], in_=S[g]["zbank", t][:], func=ACT.Identity,
+            n = SIZES[g] * P
+            nc.scalar.activation(out=buf(g, "zn")[:, t, :n], in_=G[g]["zbank", t][:, :n], func=ACT.Identity,
                                  scale=gam[:, t : t + 1], bias=bet[:, t : t + 1])
 
         def gate_mm(g, t):
-            bank = ps_g.tile([P, GTOK], F32, name="g_bank")
-            for r in range(2):
-              nc.tensor.matmul_mx(
-                out=bank[:],
-                lhsT=wg_codes[:, t * P : (t + 1) * P].bitcast(FP8X4), lhsT_scale=wg_scales[:, t * P : (t + 1) * P],
-                rhs=buf(g, "hc")[:].bitcast(FP8X4), rhs_scale=buf(g, "hsc")[:],
-                start=True, stop=True,
-            )
-            S[g]["gbank", t] = bank
+            n = SIZES[g] * P
+            bank = ps_g.tile([P, H], F32, name="g_bank")
+            for r in range(GATE_REPEAT):
+                nc.tensor.matmul_mx(
+                    out=bank[:, :n],
+                    lhsT=wg_codes[:, t * P : (t + 1) * P].bitcast(FP8X4), lhsT_scale=wg_scales[:, t * P : (t + 1) * P],
+                    rhs=buf(g, "hc")[:, :n].bitcast(FP8X4), rhs_scale=buf(g, "hsc")[:, :n],
+                    start=True, stop=True,
+                )
+            G[g]["gbank", t] = bank
 
         def gate_silu(g, t):
-            nc.scalar.activation(out=buf(g, "sg")[:, t, :], in_=S[g]["gbank", t][:], func=ACT.Silu)
+            n = SIZES[g] * P
+            nc.scalar.activation(out=buf(g, "sg")[:, t, :n], in_=G[g]["gbank", t][:, :n], func=ACT.Silu)
 
-        def product(g, i):
-            n = slice(i * 2 * P, (i + 1) * 2 * P)
+        def product(g, j):
+            n = slice(j * 256, (j + 1) * 256)
             nc.vector.tensor_tensor(
-                out=buf(g, "hb")[:, i * 2 * P * PACK : (i + 1) * 2 * P * PACK].rearrange("p (c i t) -> p c t i", i=2, t=PACK),
+                out=buf(g, "hb")[:, j * 1024 : (j + 1) * 1024].rearrange("p (c i t) -> p c t i", i=2, t=PACK),
                 in0=buf(g, "zn")[:, :, n].rearrange("p t (c i) -> p c t i", i=2),
                 in1=buf(g, "sg")[:, :, n].rearrange("p t (c i) -> p c t i", i=2),
                 op=ALU.mult,
@@ -234,66 +229,86 @@ def tile_gatedlinearattention_pb_t_kernel(tc, z, hs_bytes, hs_scale, Wg, Wo, gam
                 rhs=wo_codes[:].bitcast(FP8X4), rhs_scale=wo_scales[:],
                 start=True, stop=True,
             )
-            S[g]["obank", i] = bank
+            G[g]["obank", i] = bank
 
-        def out_copy(g, i, on_vector):
-            if on_vector:
-                nc.vector.tensor_copy(out=buf(g, "o")[:, i, :], in_=S[g]["obank", i][:])
+        def out_copy(g, i):
+            if (g, i) in V_COPY:
+                nc.vector.tensor_copy(out=buf(g, "o")[:, i, :], in_=G[g]["obank", i][:])
             else:
-                nc.scalar.copy(out=buf(g, "o")[:, i, :], in_=S[g]["obank", i][:])
+                nc.scalar.copy(out=buf(g, "o")[:, i, :], in_=G[g]["obank", i][:])
             if i % 2 == 1:
-                nc.sync.dma_start(out=out_v[g, :, i - 1 : i + 1, :], in_=buf(g, "o")[:, i - 1 : i + 1, :])
+                nc.sync.dma_start(out=rows(out2, g)[:, i - 1 : i + 1, :], in_=buf(g, "o")[:, i - 1 : i + 1, :])
 
-        def ok(g):
-            return 0 <= g < GROUPS
+        def size(g):
+            return SIZES[g] if 0 <= g < NG else 0
 
-        VEC = {(7, 1), (7, 3)}
+        def tiles(g, lo, hi):
+            return range(lo, min(hi, size(g)))
+
         with tc.manual_schedule():
-            for s in range(-3, GROUPS + 1):
-                for k in range(4):
-                    a = s + 2
-                    if ok(a) and k < 2:
-                        hs_turn(a, k)
-                    if ok(s + 1):
-                        z_turn(s + 1, k)
-                        gate_mm(s + 1, k)
-                    if ok(s) and k >= 2:
-                        out_mm(s, k - 2)
-                    if ok(s - 1) and k < 2:
-                        out_mm(s - 1, k + 2)
-                    if ok(a) and k == 0:
-                        moments(a)
-                    if ok(a) and k < 2 and s < 0:
-                        hs_prod(a, k)
-                    if ok(s + 3):
-                        stats(s + 3, k)
-                    if s == -2 and k == 3:
-                        quant_wg()
-                    if ok(a) and k < 2 and s >= 0:
-                        hs_prod(a, k)
-                    if ok(s) and k % 2 == 0:
-                        product(s, k // 2)
-                    if ok(a) and k >= 2:
-                        center(a, 2 * k - 4)
-                        center(a, 2 * k - 3)
-                    if ok(a) and k == 2:
-                        hs_quant(a)
-                    if ok(s) and k == 1:
-                        h_quant(s, 0)
-                    if s == 0 and k == 1:
-                        quant_wo()
-                    if ok(s) and k == 3:
-                        h_quant(s, 1)
-                    if ok(s + 3):
-                        widen(s + 3, k)
-                    if s == -3 and k == 3:
-                        prep_wg()
-                    if ok(s + 1):
-                        z_affine(s + 1, k)
-                        gate_silu(s + 1, k)
-                    if ok(s) and k >= 2:
-                        out_copy(s, k - 2, (s, k - 2) in VEC)
-                    if ok(s - 1) and k < 2:
-                        out_copy(s - 1, k + 2, (s - 1, k + 2) in VEC)
-                    if s == -2 and k == 3:
-                        prep_wo()
+            for a in range(-1, NG + 2):
+                n, d = a + 1, a - 2
+                if size(a):
+                    aggregate(a)
+                    moments(a)
+                for i in tiles(n, 0, 4):
+                    stats(n, i)
+                if a == -1:
+                    spread_scale()
+                    nc.scalar.copy(out=gam[:], in_=gam16[:])
+                    nc.scalar.copy(out=bet[:], in_=bet16[:])
+                for j in range(size(d) // 2):
+                    product(d, j)
+                if size(d):
+                    h_quant(d, 0)
+                    out_mm(d, 0)
+                    out_mm(d, 1)
+                    out_copy(d, 0)
+                    out_copy(d, 1)
+                if a == 0:
+                    prep_wg(0)
+                    prep_wg(1)
+                for i in tiles(a, 0, 4):
+                    center(a, i)
+                if size(a):
+                    z_turn(a, 0)
+                    z_turn(a, 1)
+                    z_affine(a, 0)
+                    z_affine(a, 1)
+                if size(d) > 2:
+                    h_quant(d, 1)
+                    out_mm(d, 2)
+                    out_copy(d, 2)
+                for i in tiles(n, 0, 3):
+                    hs_prod(n, i)
+                if a == 0:
+                    quant_wg()
+                if size(n):
+                    hs_turn(n, 0)
+                    hs_copy(n, 0)
+                if size(a):
+                    z_turn(a, 2)
+                    z_affine(a, 2)
+                    hs_quant(a)
+                    gate_mm(a, 0)
+                    gate_mm(a, 1)
+                    gate_silu(a, 0)
+                    gate_silu(a, 1)
+                if size(d) > 2:
+                    out_mm(d, 3)
+                    out_copy(d, 3)
+                if size(a):
+                    z_turn(a, 3)
+                    z_affine(a, 3)
+                    gate_mm(a, 2)
+                    gate_mm(a, 3)
+                    gate_silu(a, 2)
+                    gate_silu(a, 3)
+                for i in tiles(n, 3, 4):
+                    hs_prod(n, i)
+                if size(n) > 2:
+                    hs_turn(n, 1)
+                    hs_copy(n, 1)
+                if a == 1:
+                    prep_wo()
+                    quant_wo()

@@ -20,9 +20,9 @@ PACK = 4
 EPS = 1e-5
 SIZES = [2, 4, 4, 4, 4, 4, 4, 4, 2]
 NG = len(SIZES)
-S_CENTER = 8
+S_CENTER = 2
 GATE_REPEAT = 2
-V_COPY = {(8, 1)}
+V_COPY = {(8, 1), (7, 3)}
 
 
 def tile_gatedlinearattention_pb_t_kernel(tc, z, hs_bytes, hs_scale, Wg, Wo, gamma, beta, out):
@@ -59,8 +59,11 @@ def tile_gatedlinearattention_pb_t_kernel(tc, z, hs_bytes, hs_scale, Wg, Wo, gam
             z_t.append(z_b)
         nc.scalar.dma_start(out=sc4[:], in_=hs_scale.rearrange("a b (p j) -> (a b p) j", j=PACK))
         for g in range(NG):
+            if g == 0:
+                nc.sync.dma_start(out=hs_t[g][:], in_=rows(hs2, g))
             nc.sync.dma_start(out=z_t[g][:], in_=rows(z2, g))
-            nc.sync.dma_start(out=hs_t[g][:], in_=rows(hs2, g))
+            if g > 0:
+                nc.sync.dma_start(out=hs_t[g][:], in_=rows(hs2, g))
             if g == 0:
                 nc.sync.dma_start(out=wg_raw[:], in_=Wg.rearrange("(p j) c -> p j c", j=PACK))
                 nc.scalar.dma_start(out=gam16[:], in_=gamma.rearrange("(p j) -> p j", j=PACK))
@@ -78,7 +81,6 @@ def tile_gatedlinearattention_pb_t_kernel(tc, z, hs_bytes, hs_scale, Wg, Wo, gam
         nc.scalar.activation(out=dummy2[:], in_=dummy[:], func=ACT.Silu)
         gam = keep.tile([P, PACK], F32, name="gam")
         bet = keep.tile([P, PACK], F32, name="bet")
-        sc_t = keep.tile([P, H], F32, name="sc_t", align_bytes=64)
 
         wg_grp = keep.tile([P, H * PACK], BF16, name="wg_grp", align_bytes=64)
         wo_grp = keep.tile([P, H * PACK], BF16, name="wo_grp", align_bytes=64)
@@ -87,11 +89,7 @@ def tile_gatedlinearattention_pb_t_kernel(tc, z, hs_bytes, hs_scale, Wg, Wo, gam
         wo_codes = keep.tile([P, H], U32, name="wo_codes", align_bytes=64)
         wo_scales = keep.tile([P, H], U8, name="wo_scales", align_bytes=64)
 
-        def spread_scale():
-            bank = ps_hs.tile([P, PACK, P], F32, name="hs_bank")
-            for j in range(PACK):
-                nc.tensor.transpose(bank[:, j, :], sc4[:, j : j + 1].to_broadcast([P, P]), ident[:])
-            nc.scalar.copy(out=sc_t[:].rearrange("p (n j) -> p n j", j=PACK), in_=bank[:].rearrange("p j n -> p n j"))
+        sc_b = sc4[:].rearrange("p (u e) -> p u e", u=2).unsqueeze(1).to_broadcast([P, 256, 2, 2])
 
         def prep_wg(h):
             nc.scalar.copy(
@@ -114,8 +112,8 @@ def tile_gatedlinearattention_pb_t_kernel(tc, z, hs_bytes, hs_scale, Wg, Wo, gam
 
         G = [dict() for g in range(NG)]
         shapes = {
-            "hsm": ([P, 4, H], BF16), "hsb": ([P, 4 * H], BF16), "hc": ([P, H], U32), "hsc": ([P, H], U8),
-            "st": ([P, 4, 6], F32), "nm": ([P, 4], F32), "rs": ([P, 4], F32), "nr": ([P, 4], F32), "mv": ([P, 4, 2], F32), "ve": ([P, 4], F32),
+            "wide": ([P, 4, H], BF16), "hsb": ([P, 4 * H], BF16), "hc": ([P, H], U32), "hsc": ([P, H], U8),
+            "st": ([P, 4, 6], F32), "nm": ([P, 4], F32), "rs": ([P, 4], F32), "nr": ([P, 4], F32), "tm": ([P, 6, 4], F32), "sy": ([P, 1], F32),
             "zh": ([P, 4, PACK, P], F32), "sg": ([P, PACK, H], F32), "zn": ([P, PACK, H], F32),
             "hb": ([P, 4 * H], BF16), "c2": ([P, H], U32), "s2": ([P, H], U8), "o": ([P, 4, H], F32),
         }
@@ -133,20 +131,24 @@ def tile_gatedlinearattention_pb_t_kernel(tc, z, hs_bytes, hs_scale, Wg, Wo, gam
         def on_scalar(g, i):
             return starts[g] // P + i < S_CENTER
 
-        def aggregate(g):
-            for i in range(SIZES[g]):
-                nc.vector.bn_aggr(out=buf(g, "mv")[:, i, :], in_=buf(g, "st")[:, i, :])
-
         def moments(g):
             n = SIZES[g]
-            mean, var = buf(g, "mv")[:, :n, 0], buf(g, "mv")[:, :n, 1]
-            ve, rs = buf(g, "ve")[:, :n], buf(g, "rs")[:, :n]
-            nc.gpsimd.tensor_scalar(out=ve, in0=var, scalar1=1.0, scalar2=EPS, op0=ALU.mult, op1=ALU.add)
-            nc.gpsimd.tensor_tensor(out=rs, in0=ve, in1=mhalf[:, :n], op=ALU.pow)
+            st, tm = buf(g, "st"), buf(g, "tm")
+            me, ve, mo, vo = st[:, :n, 1], st[:, :n, 2], st[:, :n, 4], st[:, :n, 5]
+            nm, rs = buf(g, "nm")[:, :n], buf(g, "rs")[:, :n]
+            gp = nc.gpsimd
+            if 0 < g < NG - 1:
+                gp.tensor_copy(out=buf(g, "sy")[:], in_=buf(g + 1, "st")[:, 0, 0:1])
+            gp.tensor_tensor(out=tm[:, 0, :n], in0=me, in1=mo, op=ALU.add)
+            gp.tensor_tensor(out=tm[:, 1, :n], in0=me, in1=mo, op=ALU.subtract)
+            gp.tensor_tensor(out=tm[:, 2, :n], in0=ve, in1=vo, op=ALU.add)
+            gp.tensor_scalar(out=nm, in0=tm[:, 0, :n], scalar1=-0.5, scalar2=0.0, op0=ALU.mult, op1=ALU.add)
+            gp.tensor_tensor(out=tm[:, 3, :n], in0=tm[:, 1, :n], in1=tm[:, 1, :n], op=ALU.mult)
+            gp.tensor_scalar(out=tm[:, 4, :n], in0=tm[:, 2, :n], scalar1=4.0 / H, scalar2=4.0 * EPS, op0=ALU.mult, op1=ALU.add)
+            gp.tensor_tensor(out=tm[:, 5, :n], in0=tm[:, 3, :n], in1=tm[:, 4, :n], op=ALU.add)
+            gp.tensor_tensor(out=rs, in0=tm[:, 5, :n], in1=mhalf[:, :n], op=ALU.pow)
             if on_scalar(g, 0):
-                nm, nr = buf(g, "nm")[:, :n], buf(g, "nr")[:, :n]
-                nc.gpsimd.tensor_scalar(out=nm, in0=mean, scalar1=-1.0, scalar2=0.0, op0=ALU.mult, op1=ALU.add)
-                nc.gpsimd.tensor_tensor(out=nr, in0=nm, in1=rs, op=ALU.mult)
+                gp.tensor_tensor(out=buf(g, "nr")[:, :n], in0=nm, in1=rs, op=ALU.mult)
 
         def center(g, i):
             src = z_t[g][:, i, :].rearrange("p (m t) -> p t m", t=PACK)
@@ -155,24 +157,26 @@ def tile_gatedlinearattention_pb_t_kernel(tc, z, hs_bytes, hs_scale, Wg, Wo, gam
                 nc.scalar.activation(out=dst, in_=src, func=ACT.Identity,
                                      scale=buf(g, "rs")[:, i : i + 1], bias=buf(g, "nr")[:, i : i + 1])
             else:
-                nc.vector.tensor_scalar(out=dst, in0=src, scalar1=buf(g, "mv")[:, i, 0:1], scalar2=buf(g, "rs")[:, i : i + 1],
-                                        op0=ALU.subtract, op1=ALU.mult)
+                nc.vector.tensor_scalar(out=dst, in0=src, scalar1=buf(g, "nm")[:, i : i + 1], scalar2=buf(g, "rs")[:, i : i + 1],
+                                        op0=ALU.add, op1=ALU.mult)
 
-        def hs_prod(g, i):
-            nc.vector.tensor_tensor(out=buf(g, "hsm")[:, i, :], in0=hs_t[g][:, i, :].bitcast(FP8), in1=sc_t[:], op=ALU.mult)
+        def widen(g, i):
+            nc.scalar.copy(out=buf(g, "wide")[:, i, :], in_=hs_t[g][:, i, :].bitcast(FP8))
 
         def hs_turn(g, h):
             bank = ps_hs.tile([P, 2, 256], F32, name="hs_bank")
             for i in range(2):
-                words = buf(g, "hsm")[:, 2 * h + i, :].bitcast(F32)
+                words = buf(g, "wide")[:, 2 * h + i, :].bitcast(F32)
                 for u in range(2):
                     nc.tensor.transpose(bank[:, u, i * P : (i + 1) * P], words[:, u:256:2], ident[:])
             G[g]["hbank", h] = bank
 
-        def hs_copy(g, h):
-            nc.scalar.copy(
-                out=buf(g, "hsb")[:, h * 1024 : (h + 1) * 1024].bitcast(F32).rearrange("p (n u) -> p n u", u=2),
-                in_=G[g]["hbank", h][:].rearrange("p u n -> p n u"),
+        def hs_prod(g, h):
+            nc.vector.tensor_tensor(
+                out=buf(g, "hsb")[:, h * 1024 : (h + 1) * 1024].rearrange("p (n u e) -> p n u e", u=2, e=2),
+                in0=G[g]["hbank", h][:].bitcast(BF16).rearrange("p u (n e) -> p n u e", e=2),
+                in1=sc_b,
+                op=ALU.mult,
             )
 
         def hs_quant(g):
@@ -246,69 +250,52 @@ def tile_gatedlinearattention_pb_t_kernel(tc, z, hs_bytes, hs_scale, Wg, Wo, gam
             return range(lo, min(hi, size(g)))
 
         with tc.manual_schedule():
-            for a in range(-1, NG + 2):
-                n, d = a + 1, a - 2
-                if size(a):
-                    aggregate(a)
-                    moments(a)
-                for i in tiles(n, 0, 4):
-                    stats(n, i)
-                if a == -1:
-                    spread_scale()
-                    nc.scalar.copy(out=gam[:], in_=gam16[:])
-                    nc.scalar.copy(out=bet[:], in_=bet16[:])
-                for j in range(size(d) // 2):
-                    product(d, j)
-                if size(d):
-                    h_quant(d, 0)
-                    out_mm(d, 0)
-                    out_mm(d, 1)
-                    out_copy(d, 0)
-                    out_copy(d, 1)
-                if a == 0:
-                    prep_wg(0)
-                    prep_wg(1)
-                for i in tiles(a, 0, 4):
-                    center(a, i)
-                if size(a):
-                    z_turn(a, 0)
-                    z_turn(a, 1)
-                    z_affine(a, 0)
-                    z_affine(a, 1)
-                if size(d) > 2:
-                    h_quant(d, 1)
-                    out_mm(d, 2)
-                    out_copy(d, 2)
-                for i in tiles(n, 0, 3):
-                    hs_prod(n, i)
-                if a == 0:
-                    quant_wg()
-                if size(n):
-                    hs_turn(n, 0)
-                    hs_copy(n, 0)
-                if size(a):
-                    z_turn(a, 2)
-                    z_affine(a, 2)
-                    hs_quant(a)
-                    gate_mm(a, 0)
-                    gate_mm(a, 1)
-                    gate_silu(a, 0)
-                    gate_silu(a, 1)
-                if size(d) > 2:
-                    out_mm(d, 3)
-                    out_copy(d, 3)
-                if size(a):
-                    z_turn(a, 3)
-                    z_affine(a, 3)
-                    gate_mm(a, 2)
-                    gate_mm(a, 3)
-                    gate_silu(a, 2)
-                    gate_silu(a, 3)
-                for i in tiles(n, 3, 4):
-                    hs_prod(n, i)
-                if size(n) > 2:
-                    hs_turn(n, 1)
-                    hs_copy(n, 1)
-                if a == 1:
-                    prep_wo()
-                    quant_wo()
+            for s in range(-3, NG + 1):
+                l, a, b = s + 3, s + 2, s + 1
+                for k in range(4):
+                    if 2 * k < size(a):
+                        hs_turn(a, k)
+                    if size(b):
+                        z_turn(b, k)
+                        gate_mm(b, k)
+                    if k >= 2 and size(s):
+                        out_mm(s, k - 2)
+                    if k < 2 and k + 2 < size(s - 1):
+                        out_mm(s - 1, k + 2)
+                    early = (0, 1) if k == 0 else (k,) if k >= 2 else ()
+                    for i in early:
+                        if i < size(l):
+                            stats(l, i)
+                        if i == 0 and size(a):
+                            moments(a)
+                    if s == -2 and k == 3:
+                        quant_wg()
+                    if 2 * k < size(a):
+                        hs_prod(a, k)
+                    if k % 2 == 0 and k < size(s):
+                        product(s, k // 2)
+                    if k >= 2:
+                        for i in tiles(a, 2 * k - 4, 2 * k - 2):
+                            center(a, i)
+                    if k == 2 and size(a):
+                        hs_quant(a)
+                    if k % 2 == 1 and k < size(s):
+                        h_quant(s, k // 2)
+                    if s == 0 and k == 0:
+                        quant_wo()
+                    if k < size(l):
+                        widen(l, k)
+                    if s == -3 and k == 1:
+                        nc.scalar.activation(out=gam[:], in_=gam16[:], func=ACT.Copy, scale=2.0)
+                        nc.scalar.copy(out=bet[:], in_=bet16[:])
+                        prep_wg(0)
+                        prep_wg(1)
+                    if size(b):
+                        z_affine(b, k)
+                        gate_silu(b, k)
+                    if k >= 2 and size(s):
+                        out_copy(s, k - 2)
+                    if k < 2 and k + 2 < size(s - 1):
+                        out_copy(s - 1, k + 2)
+                    if s == -2 and k == 3:
+                        prep_wo()

from contextlib import ExitStack

import concourse.mybir as mybir
from concourse.masks import make_identity

TOKENS, H = 4096, 512
FLOPS = 2 * 2 * TOKENS * H * H

F32 = mybir.dt.float32
BF16 = mybir.dt.bfloat16
U32 = mybir.dt.uint32
U8 = mybir.dt.uint8
FP8 = mybir.dt.float8_e4m3fn
FP8X4 = mybir.dt.float8_e4m3fn_x4
ACT = mybir.ActivationFunctionType
ALU = mybir.AluOpType

P = 128
PACK = 4
EPS = 1e-5
SIZES = [2, 4, 4, 4, 4, 4, 4, 4, 2]
NG = len(SIZES)
S_CENTER = 2
GATE_REPEAT = 2
V_COPY = {(8, 1), (7, 3)}


def tile_gatedlinearattention_pb_t_kernel(tc, z, hs_bytes, hs_scale, Wg, Wo, gamma, beta, out):
    nc = tc.nc
    z2 = z.flatten_outer_dims()
    hs2 = hs_bytes.flatten_outer_dims()
    out2 = out.flatten_outer_dims()
    starts = [sum(SIZES[:g]) * P for g in range(NG)]

    def rows(x, g):
        n = SIZES[g]
        return x[starts[g] : starts[g] + n * P, :].rearrange("(p i) d -> p i d", i=n)

    with ExitStack() as ctx:
        keep = ctx.enter_context(tc.tile_pool(name="keep", bufs=1))
        inp = ctx.enter_context(tc.tile_pool(name="inp", bufs=NG))
        work = ctx.enter_context(tc.tile_pool(name="work", bufs=3))
        outp = ctx.enter_context(tc.tile_pool(name="outp", bufs=3))
        ps_hs = ctx.enter_context(tc.psum_pool(name="ps_hs", bufs=2))
        ps_g = ctx.enter_context(tc.psum_pool(name="ps_g", bufs=2))
        ps_z = ctx.enter_context(tc.psum_pool(name="ps_z", bufs=2))
        ps_o = ctx.enter_context(tc.psum_pool(name="ps_o", bufs=2))

        sc4 = keep.tile([P, PACK], F32, name="sc4")
        gam16 = keep.tile([P, PACK], BF16, name="gam16")
        bet16 = keep.tile([P, PACK], BF16, name="bet16")
        wg_raw = keep.tile([P, PACK, H], BF16, name="wg_raw", align_bytes=64)
        wo_raw = keep.tile([P, PACK, H], BF16, name="wo_raw", align_bytes=64)
        hs_t, z_t = [], []
        for g in range(NG):
            hs_b = inp.tile([P, SIZES[g], H], U8, name="hs_b", align_bytes=64)
            z_b = inp.tile([P, SIZES[g], H], BF16, name="z_b", align_bytes=64)
            hs_t.append(hs_b)
            z_t.append(z_b)
        nc.scalar.dma_start(out=sc4[:], in_=hs_scale.rearrange("a b (p j) -> (a b p) j", j=PACK))
        for g in range(NG):
            if g == 0:
                nc.sync.dma_start(out=hs_t[g][:], in_=rows(hs2, g))
            nc.sync.dma_start(out=z_t[g][:], in_=rows(z2, g))
            if g > 0:
                nc.sync.dma_start(out=hs_t[g][:], in_=rows(hs2, g))
            if g == 0:
                nc.sync.dma_start(out=wg_raw[:], in_=Wg.rearrange("(p j) c -> p j c", j=PACK))
                nc.scalar.dma_start(out=gam16[:], in_=gamma.rearrange("(p j) -> p j", j=PACK))
                nc.scalar.dma_start(out=bet16[:], in_=beta.rearrange("(p j) -> p j", j=PACK))
            if g == 1:
                nc.sync.dma_start(out=wo_raw[:], in_=Wo.rearrange("(p j) c -> p j c", j=PACK))

        ident = keep.tile([P, P], F32, name="ident")
        make_identity(nc, ident[:])
        mhalf = keep.tile([P, PACK], F32, name="mhalf")
        nc.gpsimd.memset(mhalf[:], -0.5)
        dummy = keep.tile([P, 1], F32, name="dummy")
        nc.vector.memset(dummy[:], 0.0)
        dummy2 = keep.tile([P, 1], F32, name="dummy2")
        nc.scalar.activation(out=dummy2[:], in_=dummy[:], func=ACT.Silu)
        gam = keep.tile([P, PACK], F32, name="gam")
        bet = keep.tile([P, PACK], F32, name="bet")

        wg_grp = keep.tile([P, H * PACK], BF16, name="wg_grp", align_bytes=64)
        wo_grp = keep.tile([P, H * PACK], BF16, name="wo_grp", align_bytes=64)
        wg_codes = keep.tile([P, H], U32, name="wg_codes", align_bytes=64)
        wg_scales = keep.tile([P, H], U8, name="wg_scales", align_bytes=64)
        wo_codes = keep.tile([P, H], U32, name="wo_codes", align_bytes=64)
        wo_scales = keep.tile([P, H], U8, name="wo_scales", align_bytes=64)

        sc_b = sc4[:].rearrange("p (u e) -> p u e", u=2).unsqueeze(1).to_broadcast([P, 256, 2, 2])

        def prep_wg(h):
            nc.scalar.copy(
                out=wg_grp[:, h * 1024 : (h + 1) * 1024].rearrange("p (t m j) -> p t m j", t=2, j=PACK),
                in_=wg_raw[:].rearrange("p j (m t) -> p t m j", t=PACK)[:, 2 * h : 2 * h + 2],
            )

        def quant_wg():
            nc.vector.quantize_mx(out=wg_codes[:].bitcast(FP8X4), scales=wg_scales[:], in_=wg_grp[:])

        def prep_wo():
            nc.gpsimd.tensor_scalar(
                out=wo_grp[:].rearrange("p (n j) -> p n j", j=PACK),
                in0=wo_raw[:].rearrange("p j n -> p n j"),
                scalar1=1.0, scalar2=0.0, op0=ALU.mult, op1=ALU.add,
            )

        def quant_wo():
            nc.vector.quantize_mx(out=wo_codes[:].bitcast(FP8X4), scales=wo_scales[:], in_=wo_grp[:])

        G = [dict() for g in range(NG)]
        shapes = {
            "wide": ([P, 4, H], BF16), "hsb": ([P, 4 * H], BF16), "hc": ([P, H], U32), "hsc": ([P, H], U8),
            "st": ([P, 4, 6], F32), "nm": ([P, 4], F32), "rs": ([P, 4], F32), "nr": ([P, 4], F32), "tm": ([P, 6, 4], F32), "sy": ([P, 1], F32),
            "zh": ([P, 4, PACK, P], F32), "sg": ([P, PACK, H], F32), "zn": ([P, PACK, H], F32),
            "hb": ([P, 4 * H], BF16), "c2": ([P, H], U32), "s2": ([P, H], U8), "o": ([P, 4, H], F32),
        }

        def buf(g, key):
            if key not in G[g]:
                shape, dt = shapes[key]
                pool = outp if key == "o" else work
                G[g][key] = pool.tile(shape, dt, name=key, align_bytes=64)
            return G[g][key]

        def stats(g, i):
            nc.vector.bn_stats(out=buf(g, "st")[:, i, :], in_=z_t[g][:, i, :])

        def on_scalar(g, i):
            return starts[g] // P + i < S_CENTER

        def moments(g):
            n = SIZES[g]
            st, tm = buf(g, "st"), buf(g, "tm")
            me, ve, mo, vo = st[:, :n, 1], st[:, :n, 2], st[:, :n, 4], st[:, :n, 5]
            nm, rs = buf(g, "nm")[:, :n], buf(g, "rs")[:, :n]
            gp = nc.gpsimd
            if 0 < g < NG - 1:
                gp.tensor_copy(out=buf(g, "sy")[:], in_=buf(g + 1, "st")[:, 0, 0:1])
            gp.tensor_tensor(out=tm[:, 0, :n], in0=me, in1=mo, op=ALU.add)
            gp.tensor_tensor(out=tm[:, 1, :n], in0=me, in1=mo, op=ALU.subtract)
            gp.tensor_tensor(out=tm[:, 2, :n], in0=ve, in1=vo, op=ALU.add)
            gp.tensor_scalar(out=nm, in0=tm[:, 0, :n], scalar1=-0.5, scalar2=0.0, op0=ALU.mult, op1=ALU.add)
            gp.tensor_tensor(out=tm[:, 3, :n], in0=tm[:, 1, :n], in1=tm[:, 1, :n], op=ALU.mult)
            gp.tensor_scalar(out=tm[:, 4, :n], in0=tm[:, 2, :n], scalar1=4.0 / H, scalar2=4.0 * EPS, op0=ALU.mult, op1=ALU.add)
            gp.tensor_tensor(out=tm[:, 5, :n], in0=tm[:, 3, :n], in1=tm[:, 4, :n], op=ALU.add)
            gp.tensor_tensor(out=rs, in0=tm[:, 5, :n], in1=mhalf[:, :n], op=ALU.pow)
            if on_scalar(g, 0):
                gp.tensor_tensor(out=buf(g, "nr")[:, :n], in0=nm, in1=rs, op=ALU.mult)

        def center(g, i):
            src = z_t[g][:, i, :].rearrange("p (m t) -> p t m", t=PACK)
            dst = buf(g, "zh")[:, i, :, :]
            if on_scalar(g, i):
                nc.scalar.activation(out=dst, in_=src, func=ACT.Identity,
                                     scale=buf(g, "rs")[:, i : i + 1], bias=buf(g, "nr")[:, i : i + 1])
            else:
                nc.vector.tensor_scalar(out=dst, in0=src, scalar1=buf(g, "nm")[:, i : i + 1], scalar2=buf(g, "rs")[:, i : i + 1],
                                        op0=ALU.add, op1=ALU.mult)

        def widen(g, i):
            nc.scalar.copy(out=buf(g, "wide")[:, i, :], in_=hs_t[g][:, i, :].bitcast(FP8))

        def hs_turn(g, h):
            bank = ps_hs.tile([P, 2, 256], F32, name="hs_bank")
            for i in range(2):
                words = buf(g, "wide")[:, 2 * h + i, :].bitcast(F32)
                for u in range(2):
                    nc.tensor.transpose(bank[:, u, i * P : (i + 1) * P], words[:, u:256:2], ident[:])
            G[g]["hbank", h] = bank

        def hs_prod(g, h):
            nc.vector.tensor_tensor(
                out=buf(g, "hsb")[:, h * 1024 : (h + 1) * 1024].rearrange("p (n u e) -> p n u e", u=2, e=2),
                in0=G[g]["hbank", h][:].bitcast(BF16).rearrange("p u (n e) -> p n u e", e=2),
                in1=sc_b,
                op=ALU.mult,
            )

        def hs_quant(g):
            n = SIZES[g] * P
            nc.vector.quantize_mx(out=buf(g, "hc")[:, :n].bitcast(FP8X4), scales=buf(g, "hsc")[:, :n], in_=buf(g, "hsb")[:, : 4 * n])

        def z_turn(g, t):
            bank = ps_z.tile([P, H], F32, name="z_bank")
            for i in range(SIZES[g]):
                nc.tensor.transpose(bank[:, i * P : (i + 1) * P], buf(g, "zh")[:, i, t, :], ident[:])
            G[g]["zbank", t] = bank

        def z_affine(g, t):
            n = SIZES[g] * P
            nc.scalar.activation(out=buf(g, "zn")[:, t, :n], in_=G[g]["zbank", t][:, :n], func=ACT.Identity,
                                 scale=gam[:, t : t + 1], bias=bet[:, t : t + 1])

        def gate_mm(g, t):
            n = SIZES[g] * P
            bank = ps_g.tile([P, H], F32, name="g_bank")
            for r in range(GATE_REPEAT):
                nc.tensor.matmul_mx(
                    out=bank[:, :n],
                    lhsT=wg_codes[:, t * P : (t + 1) * P].bitcast(FP8X4), lhsT_scale=wg_scales[:, t * P : (t + 1) * P],
                    rhs=buf(g, "hc")[:, :n].bitcast(FP8X4), rhs_scale=buf(g, "hsc")[:, :n],
                    start=True, stop=True,
                )
            G[g]["gbank", t] = bank

        def gate_silu(g, t):
            n = SIZES[g] * P
            nc.scalar.activation(out=buf(g, "sg")[:, t, :n], in_=G[g]["gbank", t][:, :n], func=ACT.Silu)

        def product(g, j):
            n = slice(j * 256, (j + 1) * 256)
            nc.vector.tensor_tensor(
                out=buf(g, "hb")[:, j * 1024 : (j + 1) * 1024].rearrange("p (c i t) -> p c t i", i=2, t=PACK),
                in0=buf(g, "zn")[:, :, n].rearrange("p t (c i) -> p c t i", i=2),
                in1=buf(g, "sg")[:, :, n].rearrange("p t (c i) -> p c t i", i=2),
                op=ALU.mult,
            )

        def h_quant(g, j):
            w = slice(j * 256, (j + 1) * 256)
            nc.vector.quantize_mx(out=buf(g, "c2")[:, w].bitcast(FP8X4), scales=buf(g, "s2")[:, w],
                                  in_=buf(g, "hb")[:, j * 1024 : (j + 1) * 1024])

        def out_mm(g, i):
            n = slice(i * P, (i + 1) * P)
            bank = ps_o.tile([P, H], F32, name="o_bank")
            nc.tensor.matmul_mx(
                out=bank[:],
                lhsT=buf(g, "c2")[:, n].bitcast(FP8X4), lhsT_scale=buf(g, "s2")[:, n],
                rhs=wo_codes[:].bitcast(FP8X4), rhs_scale=wo_scales[:],
                start=True, stop=True,
            )
            G[g]["obank", i] = bank

        def out_copy(g, i):
            if (g, i) in V_COPY:
                nc.vector.tensor_copy(out=buf(g, "o")[:, i, :], in_=G[g]["obank", i][:])
            else:
                nc.scalar.copy(out=buf(g, "o")[:, i, :], in_=G[g]["obank", i][:])
            if i % 2 == 1:
                nc.sync.dma_start(out=rows(out2, g)[:, i - 1 : i + 1, :], in_=buf(g, "o")[:, i - 1 : i + 1, :])

        def size(g):
            return SIZES[g] if 0 <= g < NG else 0

        def tiles(g, lo, hi):
            return range(lo, min(hi, size(g)))

        with tc.manual_schedule():
            for s in range(-3, NG + 1):
                l, a, b = s + 3, s + 2, s + 1
                for k in range(4):
                    if 2 * k < size(a):
                        hs_turn(a, k)
                    if size(b):
                        z_turn(b, k)
                        gate_mm(b, k)
                    if k >= 2 and size(s):
                        out_mm(s, k - 2)
                    if k < 2 and k + 2 < size(s - 1):
                        out_mm(s - 1, k + 2)
                    early = (0, 1) if k == 0 else (k,) if k >= 2 else ()
                    for i in early:
                        if i < size(l):
                            stats(l, i)
                        if i == 0 and size(a):
                            moments(a)
                    if s == -2 and k == 3:
                        quant_wg()
                    if 2 * k < size(a):
                        hs_prod(a, k)
                    if k % 2 == 0 and k < size(s):
                        product(s, k // 2)
                    if k >= 2:
                        for i in tiles(a, 2 * k - 4, 2 * k - 2):
                            center(a, i)
                    if k == 2 and size(a):
                        hs_quant(a)
                    if k % 2 == 1 and k < size(s):
                        h_quant(s, k // 2)
                    if s == 0 and k == 0:
                        quant_wo()
                    if k < size(l):
                        widen(l, k)
                    if s == -3 and k == 1:
                        nc.scalar.activation(out=gam[:], in_=gam16[:], func=ACT.Copy, scale=2.0)
                        nc.scalar.copy(out=bet[:], in_=bet16[:])
                        prep_wg(0)
                        prep_wg(1)
                    if size(b):
                        z_affine(b, k)
                        gate_silu(b, k)
                    if k >= 2 and size(s):
                        out_copy(s, k - 2)
                    if k < 2 and k + 2 < size(s - 1):
                        out_copy(s - 1, k + 2)
                    if s == -2 and k == 3:
                        prep_wo()
